import numpy as np
import ml_dtypes


def mxq(x, axis, fmt="e4m3"):
    dtype, down = {"e4m3": (ml_dtypes.float8_e4m3fn, 7), "e5m2": (ml_dtypes.float8_e5m2, 14)}[fmt]
    v = np.moveaxis(np.asarray(x, np.float32).astype(ml_dtypes.bfloat16).astype(np.float64), axis, -1)
    blocks = v.reshape(v.shape[:-1] + (-1, 32))
    amax = np.abs(blocks).max(-1, keepdims=True)
    byte = np.maximum(np.where(amax > 0, np.frexp(amax)[1] - 1 + 127, 0) - down, 1)
    scale = np.exp2(byte - 127.0)
    codes = (blocks / scale).astype(np.float32).astype(dtype).astype(np.float64)
    return np.moveaxis((codes * scale).reshape(v.shape), -1, axis)


WIDE = False


def mx_kscale(k):
    if not WIDE:
        return np.ones(k)
    levels = np.array([10, -10, 5, -5, 0])
    a = np.random.permutation(np.resize(levels, k // 512 * 4)).reshape(k // 512, 4)
    idx = np.arange(k)
    return np.exp2(a[idx // 512, idx % 128 // 32])


BF16 = ml_dtypes.bfloat16


def bf(x):
    return np.asarray(x, np.float32).astype(BF16)


def f64(x):
    return np.asarray(x).astype(np.float64)


B, S, D, F, G, K = 2, 64, 512, 1024, 1, 1
N = B * S
NB = G + K
C = D * NB


def silu(v):
    e = np.exp(-np.abs(v))
    return v * np.where(v >= 0, 1.0, e) / (1.0 + e)


def b_splines(x, grid, k):
    x = x[..., None]
    bases = np.where((x >= grid[:-1]) & (x < grid[1:]), 1.0, 0.0)
    for j in range(1, k + 1):
        left = (x - grid[: -(j + 1)]) / (grid[j:-1] - grid[: -(j + 1)])
        right = (grid[j + 1:] - x) / (grid[j + 1:] - grid[1:-j])
        bases = left * bases[..., :-1] + right * bases[..., 1:]
    return bases


def setup_inputs():
    t = np.maximum(mx_kscale(D), 1.0) ** 2
    return {"x": bf(np.random.standard_normal((B, S, D)) * t),
            "grid": bf(np.arange(-K, G + K + 1) * (2.0 / G) - 1.0),
            "w1_base": bf(np.random.standard_normal((F, D)) / np.sqrt(D) / t),
            "w1_spline": bf(np.random.standard_normal((F, D, NB)) / np.sqrt(D))}


def reference(x, grid, w1_base, w1_spline):
    xf = f64(x).reshape(N, D)
    base = mxq(silu(xf), 1, "e4m3") @ mxq(f64(w1_base), 1, "e4m3").T
    bases = b_splines(xf, f64(grid), K).reshape(N, C)
    spline = mxq(bases, 1, "e4m3") @ mxq(f64(w1_spline).reshape(F, C), 1, "e4m3").T
    return base + spline

@@ -1,0 +1,201 @@
+from contextlib import ExitStack
+
+import concourse.mybir as mybir
+from concourse.masks import make_identity
+
+BF16 = mybir.dt.bfloat16
+F32 = mybir.dt.float32
+U32 = mybir.dt.uint32
+U8 = mybir.dt.uint8
+FP8X4 = mybir.dt.float8_e4m3fn_x4
+ACT = mybir.ActivationFunctionType
+ALU = mybir.AluOpType
+
+P = 128
+PACK = 4
+HALVES = 2
+D = 512
+BASES = 2
+SPLINE_PASSES = D * BASES // (P * PACK)
+F = 1024
+ROWS = 2
+F_ROUND = ROWS * P
+ROUNDS = F // F_ROUND
+BANK = 512
+
+FLOPS = 2 * P * F * (D + D * BASES)
+
+
+def tile_kanblock_pa_s_kernel(tc, x, grid, w1_base, w1_spline, out):
+    nc = tc.nc
+    x_rows = x.flatten_outer_dims()
+    base_rounds = w1_base.rearrange("(r p a) k -> r p (a k)", p=P, a=ROWS)
+    spline_rounds = w1_spline.rearrange("(r p a) i g -> r p (a i g)", p=P, a=ROWS)
+
+    with ExitStack() as stack:
+        const = stack.enter_context(tc.tile_pool(name="const", bufs=1))
+        weights = stack.enter_context(tc.tile_pool(name="weights", bufs=ROUNDS))
+        work = stack.enter_context(tc.tile_pool(name="work", bufs=2))
+        spline_banks = stack.enter_context(tc.psum_pool(name="spline_banks", bufs=2 * ROWS))
+        base_banks = stack.enter_context(tc.psum_pool(name="base_banks", bufs=2))
+        product_banks = stack.enter_context(tc.psum_pool(name="product_banks", bufs=2))
+
+        x_sb = const.tile([P, D], BF16)
+        nc.sync.dma_start(out=x_sb[:], in_=x_rows)
+        knots_bf = const.tile([P, 4], BF16)
+        nc.scalar.dma_start(out=knots_bf[:], in_=grid.partition_broadcast(P))
+        base_rows = []
+        spline_rows = []
+        for r in range(ROUNDS):
+            base_sb = weights.tile([P, ROWS * D], BF16)
+            nc.sync.dma_start(out=base_sb[:], in_=base_rounds[r])
+            base_rows.append(base_sb)
+            spline_sb = weights.tile([P, ROWS * D * BASES], BF16)
+            nc.sync.dma_start(out=spline_sb[:], in_=spline_rounds[r])
+            spline_rows.append(spline_sb)
+
+        warm = const.tile([P, 1], F32)
+        nc.vector.memset(warm[:], 0.0)
+        nc.scalar.activation(out=warm[:], in_=warm[:], func=ACT.Silu)
+        ident_f32 = const.tile([P, P], F32)
+        make_identity(nc, ident_f32[:])
+        ident_bf16 = const.tile([P, P], BF16)
+        make_identity(nc, ident_bf16[:])
+
+        knots = const.tile([P, 4], F32)
+        nc.vector.tensor_copy(out=knots[:], in_=knots_bf[:])
+        width = const.tile([P, 3], F32)
+        nc.vector.tensor_sub(out=width[:], in0=knots[:, 1:4], in1=knots[:, 0:3])
+        slope = const.tile([P, 3], F32)
+        nc.vector.reciprocal(out=slope[:], in_=width[:])
+        ratio = const.tile([P, BASES], F32)
+        nc.vector.scalar_tensor_tensor(
+            out=ratio[:], in0=slope[:, 1:3], scalar=-1.0, in1=width[:, 0:2], op0=ALU.mult, op1=ALU.mult
+        )
+
+        x_words = base_banks.tile([P, HALVES, P], F32, tag="base_bank")
+        for u in range(HALVES):
+            nc.tensor.transpose(x_words[:, u, :], x_sb[:].bitcast(F32)[:, u * P : (u + 1) * P], ident_f32[:])
+        silu_grouped = const.tile([P, P, PACK], BF16, align_bytes=64)
+        nc.scalar.activation(
+            out=silu_grouped[:].rearrange("p n (u e) -> p n u e", e=2),
+            in_=x_words[:].bitcast(BF16).rearrange("p u (n e) -> p n u e", e=2),
+            func=ACT.Silu,
+        )
+        silu_codes = const.tile([P, P], U32, align_bytes=64)
+        silu_scales = const.tile([P, P], U8, align_bytes=64)
+
+        x_feat = spline_banks.tile([P, SPLINE_PASSES * HALVES, P], BF16, tag="spline_bank")
+        for j in range(SPLINE_PASSES * HALVES):
+            nc.tensor.transpose(x_feat[:, j, :], x_sb[:, j * P : (j + 1) * P], ident_bf16[:])
+        bases_grouped = const.tile([P, SPLINE_PASSES, P, PACK], BF16, align_bytes=64)
+        bases_by_e = bases_grouped[:].rearrange("p g n (u e) -> p e g n u", e=BASES)
+        for e in range(BASES):
+            falling = work.tile([P, SPLINE_PASSES * HALVES, P], F32)
+            nc.vector.tensor_scalar(
+                out=falling[:],
+                in0=x_feat[:],
+                scalar1=knots[:, e + 2 : e + 3],
+                scalar2=ratio[:, e : e + 1],
+                op0=ALU.subtract,
+                op1=ALU.mult,
+            )
+            tent = work.tile([P, SPLINE_PASSES * HALVES, P], F32)
+            nc.vector.scalar_tensor_tensor(
+                out=tent[:],
+                in0=x_feat[:],
+                scalar=knots[:, e : e + 1],
+                in1=falling[:],
+                op0=ALU.subtract,
+                op1=ALU.min,
+            )
+            nc.scalar.activation(
+                out=bases_by_e[:, e],
+                in_=tent[:].rearrange("p (g u) n -> p g n u", u=HALVES),
+                func=ACT.Relu,
+                scale=slope[:, e : e + 1],
+            )
+        bases_codes = const.tile([P, SPLINE_PASSES, P], U32, align_bytes=64)
+        bases_scales = const.tile([P, SPLINE_PASSES, P], U8, align_bytes=64)
+
+        nc.vector.quantize_mx(
+            out=silu_codes[:].bitcast(FP8X4),
+            scales=silu_scales[:],
+            in_=silu_grouped[:].rearrange("p n t -> p (n t)"),
+        )
+        nc.vector.quantize_mx(
+            out=bases_codes[:].rearrange("p g n -> p (g n)").bitcast(FP8X4),
+            scales=bases_scales[:].rearrange("p g n -> p (g n)"),
+            in_=bases_grouped[:].rearrange("p g n t -> p (g n t)"),
+        )
+
+        for r in range(ROUNDS):
+            base_words = base_rows[r][:].bitcast(F32)
+            base_bank = base_banks.tile([P, ROWS, HALVES, P], F32, tag="base_bank")
+            for a in range(ROWS):
+                for u in range(HALVES):
+                    w = a * HALVES + u
+                    nc.tensor.transpose(base_bank[:, a, u, :], base_words[:, w * P : (w + 1) * P], ident_f32[:])
+            spline_words = spline_rows[r][:].bitcast(F32)
+            spline_bank = []
+            for a in range(ROWS):
+                bank = spline_banks.tile([P, SPLINE_PASSES * HALVES, P], F32, tag="spline_bank")
+                for j in range(SPLINE_PASSES * HALVES):
+                    w = a * SPLINE_PASSES * HALVES + j
+                    nc.tensor.transpose(bank[:, j, :], spline_words[:, w * P : (w + 1) * P], ident_f32[:])
+                spline_bank.append(bank)
+
+            base_grouped = work.tile([P, F_ROUND, PACK], BF16, align_bytes=64)
+            nc.vector.tensor_copy(
+                out=base_grouped[:].bitcast(F32).rearrange("p (a f) u -> p a f u", a=ROWS),
+                in_=base_bank[:].rearrange("p a u f -> p a f u"),
+            )
+            spline_grouped = work.tile([P, SPLINE_PASSES, F_ROUND, PACK], BF16, align_bytes=64)
+            for a in range(ROWS):
+                nc.scalar.copy(
+                    out=spline_grouped[:].bitcast(F32)[:, :, a * P : (a + 1) * P, :],
+                    in_=spline_bank[a][:].rearrange("p (g u) f -> p g f u", u=HALVES),
+                )
+
+            base_codes = work.tile([P, F_ROUND], U32, align_bytes=64)
+            base_scales = work.tile([P, F_ROUND], U8, align_bytes=64)
+            nc.vector.quantize_mx(
+                out=base_codes[:].bitcast(FP8X4),
+                scales=base_scales[:],
+                in_=base_grouped[:].rearrange("p f t -> p (f t)"),
+            )
+            spline_codes = work.tile([P, SPLINE_PASSES, F_ROUND], U32, align_bytes=64)
+            spline_scales = work.tile([P, SPLINE_PASSES, F_ROUND], U8, align_bytes=64)
+            nc.vector.quantize_mx(
+                out=spline_codes[:].rearrange("p g f -> p (g f)").bitcast(FP8X4),
+                scales=spline_scales[:].rearrange("p g f -> p (g f)"),
+                in_=spline_grouped[:].rearrange("p g f t -> p (g f t)"),
+            )
+
+            product = product_banks.tile([P, BANK], F32)
+            nc.tensor.matmul_mx(
+                out=product[:, :F_ROUND],
+                lhsT=silu_codes[:].bitcast(FP8X4),
+                lhsT_scale=silu_scales[:],
+                rhs=base_codes[:].bitcast(FP8X4),
+                rhs_scale=base_scales[:],
+                start=True,
+                stop=False,
+            )
+            for g in range(SPLINE_PASSES):
+                nc.tensor.matmul_mx(
+                    out=product[:, :F_ROUND],
+                    lhsT=bases_codes[:, g, :].bitcast(FP8X4),
+                    lhsT_scale=bases_scales[:, g, :],
+                    rhs=spline_codes[:, g, :].bitcast(FP8X4),
+                    rhs_scale=spline_scales[:, g, :],
+                    start=False,
+                    stop=(g == SPLINE_PASSES - 1),
+                )
+
+            result = work.tile([P, F_ROUND], F32)
+            nc.scalar.copy(
+                out=result[:].rearrange("n (f a) -> n f a", a=ROWS),
+                in_=product[:, :F_ROUND].rearrange("n (a f) -> n f a", a=ROWS),
+            )
+            nc.sync.dma_start(out=out[:, r * F_ROUND : (r + 1) * F_ROUND], in_=result[:])

@@ -7,6 +7,7 @@ BF16 = mybir.dt.bfloat16
 F32 = mybir.dt.float32
 U32 = mybir.dt.uint32
 U8 = mybir.dt.uint8
+I32 = mybir.dt.int32
 FP8X4 = mybir.dt.float8_e4m3fn_x4
 ACT = mybir.ActivationFunctionType
 ALU = mybir.AluOpType
@@ -22,6 +23,8 @@ ROWS = 2
 F_ROUND = ROWS * P
 ROUNDS = F // F_ROUND
 BANK = 512
+WARM_PASSES = 10
+KEEP_PASSES = 2
 
 FLOPS = 2 * P * F * (D + D * BASES)
 
@@ -36,9 +39,9 @@ def tile_kanblock_pa_s_kernel(tc, x, grid, w1_base, w1_spline, out):
         const = stack.enter_context(tc.tile_pool(name="const", bufs=1))
         weights = stack.enter_context(tc.tile_pool(name="weights", bufs=ROUNDS))
         work = stack.enter_context(tc.tile_pool(name="work", bufs=2))
-        spline_banks = stack.enter_context(tc.psum_pool(name="spline_banks", bufs=2 * ROWS))
-        base_banks = stack.enter_context(tc.psum_pool(name="base_banks", bufs=2))
+        banks = stack.enter_context(tc.psum_pool(name="banks", bufs=5))
         product_banks = stack.enter_context(tc.psum_pool(name="product_banks", bufs=2))
+        idle_banks = stack.enter_context(tc.psum_pool(name="idle_banks", bufs=1))
 
         x_sb = const.tile([P, D], BF16)
         nc.sync.dma_start(out=x_sb[:], in_=x_rows)
@@ -53,6 +56,27 @@ def tile_kanblock_pa_s_kernel(tc, x, grid, w1_base, w1_spline, out):
             spline_sb = weights.tile([P, ROWS * D * BASES], BF16)
             nc.sync.dma_start(out=spline_sb[:], in_=spline_rounds[r])
             spline_rows.append(spline_sb)
+
+        idle_bank = idle_banks.tile([P, BANK], F32)
+        zeros = const.tile([P, F_ROUND * PACK], BF16, align_bytes=64)
+        nc.vector.memset(zeros[:].bitcast(I32), 0)
+        zero_codes = const.tile([P, F_ROUND], U32, align_bytes=64)
+        zero_scales = const.tile([P, F_ROUND], U8, align_bytes=64)
+        nc.vector.quantize_mx(out=zero_codes[:].bitcast(FP8X4), scales=zero_scales[:], in_=zeros[:])
+
+        def idle_passes(count, codes, scales):
+            for i in range(count):
+                nc.tensor.matmul_mx(
+                    out=idle_bank[:, :F_ROUND],
+                    lhsT=codes[:, :P].bitcast(FP8X4),
+                    lhsT_scale=scales[:, :P],
+                    rhs=codes[:].bitcast(FP8X4),
+                    rhs_scale=scales[:],
+                    start=True,
+                    stop=True,
+                )
+
+        idle_passes(WARM_PASSES, zero_codes, zero_scales)
 
         warm = const.tile([P, 1], F32)
         nc.vector.memset(warm[:], 0.0)
@@ -73,7 +97,7 @@ def tile_kanblock_pa_s_kernel(tc, x, grid, w1_base, w1_spline, out):
             out=ratio[:], in0=slope[:, 1:3], scalar=-1.0, in1=width[:, 0:2], op0=ALU.mult, op1=ALU.mult
         )
 
-        x_words = base_banks.tile([P, HALVES, P], F32, tag="base_bank")
+        x_words = banks.tile([P, HALVES, P], F32, tag="bank")
         for u in range(HALVES):
             nc.tensor.transpose(x_words[:, u, :], x_sb[:].bitcast(F32)[:, u * P : (u + 1) * P], ident_f32[:])
         silu_grouped = const.tile([P, P, PACK], BF16, align_bytes=64)
@@ -85,7 +109,7 @@ def tile_kanblock_pa_s_kernel(tc, x, grid, w1_base, w1_spline, out):
         silu_codes = const.tile([P, P], U32, align_bytes=64)
         silu_scales = const.tile([P, P], U8, align_bytes=64)
 
-        x_feat = spline_banks.tile([P, SPLINE_PASSES * HALVES, P], BF16, tag="spline_bank")
+        x_feat = banks.tile([P, SPLINE_PASSES * HALVES, P], BF16, tag="bank")
         for j in range(SPLINE_PASSES * HALVES):
             nc.tensor.transpose(x_feat[:, j, :], x_sb[:, j * P : (j + 1) * P], ident_bf16[:])
         bases_grouped = const.tile([P, SPLINE_PASSES, P, PACK], BF16, align_bytes=64)
@@ -131,7 +155,7 @@ def tile_kanblock_pa_s_kernel(tc, x, grid, w1_base, w1_spline, out):
 
         for r in range(ROUNDS):
             base_words = base_rows[r][:].bitcast(F32)
-            base_bank = base_banks.tile([P, ROWS, HALVES, P], F32, tag="base_bank")
+            base_bank = banks.tile([P, ROWS, HALVES, P], F32, tag="bank")
             for a in range(ROWS):
                 for u in range(HALVES):
                     w = a * HALVES + u
@@ -139,7 +163,7 @@ def tile_kanblock_pa_s_kernel(tc, x, grid, w1_base, w1_spline, out):
             spline_words = spline_rows[r][:].bitcast(F32)
             spline_bank = []
             for a in range(ROWS):
-                bank = spline_banks.tile([P, SPLINE_PASSES * HALVES, P], F32, tag="spline_bank")
+                bank = banks.tile([P, SPLINE_PASSES * HALVES, P], F32, tag="bank")
                 for j in range(SPLINE_PASSES * HALVES):
                     w = a * SPLINE_PASSES * HALVES + j
                     nc.tensor.transpose(bank[:, j, :], spline_words[:, w * P : (w + 1) * P], ident_f32[:])
@@ -164,6 +188,7 @@ def tile_kanblock_pa_s_kernel(tc, x, grid, w1_base, w1_spline, out):
                 scales=base_scales[:],
                 in_=base_grouped[:].rearrange("p f t -> p (f t)"),
             )
+            idle_passes(KEEP_PASSES, base_codes, base_scales)
             spline_codes = work.tile([P, SPLINE_PASSES, F_ROUND], U32, align_bytes=64)
             spline_scales = work.tile([P, SPLINE_PASSES, F_ROUND], U8, align_bytes=64)
             nc.vector.quantize_mx(

@@ -7,7 +7,6 @@ BF16 = mybir.dt.bfloat16
 F32 = mybir.dt.float32
 U32 = mybir.dt.uint32
 U8 = mybir.dt.uint8
-I32 = mybir.dt.int32
 FP8X4 = mybir.dt.float8_e4m3fn_x4
 ACT = mybir.ActivationFunctionType
 ALU = mybir.AluOpType
@@ -18,13 +17,13 @@ HALVES = 2
 D = 512
 BASES = 2
 SPLINE_PASSES = D * BASES // (P * PACK)
+BLOCKS = D // P
 F = 1024
 ROWS = 2
 F_ROUND = ROWS * P
 ROUNDS = F // F_ROUND
+LAG = 2
 BANK = 512
-WARM_PASSES = 10
-KEEP_PASSES = 2
 
 FLOPS = 2 * P * F * (D + D * BASES)
 
@@ -36,55 +35,34 @@ def tile_kanblock_pa_s_kernel(tc, x, grid, w1_base, w1_spline, out):
     spline_rounds = w1_spline.rearrange("(r p a) i g -> r p (a i g)", p=P, a=ROWS)
 
     with ExitStack() as stack:
+        stack.enter_context(tc.manual_schedule())
         const = stack.enter_context(tc.tile_pool(name="const", bufs=1))
-        weights = stack.enter_context(tc.tile_pool(name="weights", bufs=ROUNDS))
+        resident = stack.enter_context(tc.tile_pool(name="resident", bufs=ROUNDS))
         work = stack.enter_context(tc.tile_pool(name="work", bufs=2))
-        banks = stack.enter_context(tc.psum_pool(name="banks", bufs=5))
+        banks = stack.enter_context(tc.psum_pool(name="banks", bufs=6))
         product_banks = stack.enter_context(tc.psum_pool(name="product_banks", bufs=2))
-        idle_banks = stack.enter_context(tc.psum_pool(name="idle_banks", bufs=1))
 
-        x_sb = const.tile([P, D], BF16)
-        nc.sync.dma_start(out=x_sb[:], in_=x_rows)
         knots_bf = const.tile([P, 4], BF16)
         nc.scalar.dma_start(out=knots_bf[:], in_=grid.partition_broadcast(P))
+        x_sb = const.tile([P, D], BF16)
+        nc.sync.dma_start(out=x_sb[:], in_=x_rows)
         base_rows = []
         spline_rows = []
         for r in range(ROUNDS):
-            base_sb = weights.tile([P, ROWS * D], BF16)
-            nc.sync.dma_start(out=base_sb[:], in_=base_rounds[r])
-            base_rows.append(base_sb)
-            spline_sb = weights.tile([P, ROWS * D * BASES], BF16)
+            spline_sb = resident.tile([P, ROWS * D * BASES], BF16)
             nc.sync.dma_start(out=spline_sb[:], in_=spline_rounds[r])
             spline_rows.append(spline_sb)
-
-        idle_bank = idle_banks.tile([P, BANK], F32)
-        zeros = const.tile([P, F_ROUND * PACK], BF16, align_bytes=64)
-        nc.vector.memset(zeros[:].bitcast(I32), 0)
-        zero_codes = const.tile([P, F_ROUND], U32, align_bytes=64)
-        zero_scales = const.tile([P, F_ROUND], U8, align_bytes=64)
-        nc.vector.quantize_mx(out=zero_codes[:].bitcast(FP8X4), scales=zero_scales[:], in_=zeros[:])
-
-        def idle_passes(count, codes, scales):
-            for i in range(count):
-                nc.tensor.matmul_mx(
-                    out=idle_bank[:, :F_ROUND],
-                    lhsT=codes[:, :P].bitcast(FP8X4),
-                    lhsT_scale=scales[:, :P],
-                    rhs=codes[:].bitcast(FP8X4),
-                    rhs_scale=scales[:],
-                    start=True,
-                    stop=True,
-                )
-
-        idle_passes(WARM_PASSES, zero_codes, zero_scales)
+            base_sb = resident.tile([P, ROWS * D], BF16)
+            nc.sync.dma_start(out=base_sb[:], in_=base_rounds[r])
+            base_rows.append(base_sb)
 
         warm = const.tile([P, 1], F32)
         nc.vector.memset(warm[:], 0.0)
         nc.scalar.activation(out=warm[:], in_=warm[:], func=ACT.Silu)
-        ident_f32 = const.tile([P, P], F32)
-        make_identity(nc, ident_f32[:])
         ident_bf16 = const.tile([P, P], BF16)
         make_identity(nc, ident_bf16[:])
+        ident_f32 = const.tile([P, P], F32)
+        make_identity(nc, ident_f32[:])
 
         knots = const.tile([P, 4], F32)
         nc.vector.tensor_copy(out=knots[:], in_=knots_bf[:])
@@ -96,117 +74,128 @@ def tile_kanblock_pa_s_kernel(tc, x, grid, w1_base, w1_spline, out):
         nc.vector.scalar_tensor_tensor(
             out=ratio[:], in0=slope[:, 1:3], scalar=-1.0, in1=width[:, 0:2], op0=ALU.mult, op1=ALU.mult
         )
+        shift = const.tile([P, BASES], F32)
+        nc.vector.scalar_tensor_tensor(
+            out=shift[:], in0=knots[:, 2:4], scalar=-1.0, in1=ratio[:], op0=ALU.mult, op1=ALU.mult
+        )
 
-        x_words = banks.tile([P, HALVES, P], F32, tag="bank")
+        x_words = product_banks.tile([P, HALVES, P], F32, tag="product")
+        x_feat_vector = product_banks.tile([P, BLOCKS, P], BF16, tag="product")
+        x_feat_scalar = banks.tile([P, BLOCKS, P], BF16, tag="bank")
+        for x_feat in (x_feat_scalar, x_feat_vector):
+            for j in range(BLOCKS):
+                nc.tensor.transpose(x_feat[:, j, :], x_sb[:, j * P : (j + 1) * P], ident_bf16[:])
         for u in range(HALVES):
             nc.tensor.transpose(x_words[:, u, :], x_sb[:].bitcast(F32)[:, u * P : (u + 1) * P], ident_f32[:])
+
+        bases_grouped = const.tile([P, SPLINE_PASSES, P, PACK], BF16, align_bytes=64)
+        bases_by_e = bases_grouped[:].rearrange("p g n (u e) -> p e g n u", e=BASES)
+        falling = []
+        for e in range(BASES):
+            line = work.tile([P, BLOCKS, P], F32)
+            nc.scalar.activation(
+                out=line[:],
+                in_=x_feat_scalar[:],
+                func=ACT.Identity,
+                scale=ratio[:, e : e + 1],
+                bias=shift[:, e : e + 1],
+            )
+            falling.append(line)
         silu_grouped = const.tile([P, P, PACK], BF16, align_bytes=64)
         nc.scalar.activation(
             out=silu_grouped[:].rearrange("p n (u e) -> p n u e", e=2),
             in_=x_words[:].bitcast(BF16).rearrange("p u (n e) -> p n u e", e=2),
             func=ACT.Silu,
         )
-        silu_codes = const.tile([P, P], U32, align_bytes=64)
-        silu_scales = const.tile([P, P], U8, align_bytes=64)
-
-        x_feat = banks.tile([P, SPLINE_PASSES * HALVES, P], BF16, tag="bank")
-        for j in range(SPLINE_PASSES * HALVES):
-            nc.tensor.transpose(x_feat[:, j, :], x_sb[:, j * P : (j + 1) * P], ident_bf16[:])
-        bases_grouped = const.tile([P, SPLINE_PASSES, P, PACK], BF16, align_bytes=64)
-        bases_by_e = bases_grouped[:].rearrange("p g n (u e) -> p e g n u", e=BASES)
         for e in range(BASES):
-            falling = work.tile([P, SPLINE_PASSES * HALVES, P], F32)
-            nc.vector.tensor_scalar(
-                out=falling[:],
-                in0=x_feat[:],
-                scalar1=knots[:, e + 2 : e + 3],
-                scalar2=ratio[:, e : e + 1],
-                op0=ALU.subtract,
-                op1=ALU.mult,
-            )
-            tent = work.tile([P, SPLINE_PASSES * HALVES, P], F32)
+            tent = work.tile([P, BLOCKS, P], F32)
             nc.vector.scalar_tensor_tensor(
                 out=tent[:],
-                in0=x_feat[:],
+                in0=x_feat_vector[:],
                 scalar=knots[:, e : e + 1],
-                in1=falling[:],
+                in1=falling[e][:],
                 op0=ALU.subtract,
                 op1=ALU.min,
             )
-            nc.scalar.activation(
+            nc.vector.tensor_scalar(
                 out=bases_by_e[:, e],
-                in_=tent[:].rearrange("p (g u) n -> p g n u", u=HALVES),
-                func=ACT.Relu,
-                scale=slope[:, e : e + 1],
+                in0=tent[:].rearrange("p (g u) n -> p g n u", u=HALVES),
+                scalar1=slope[:, e : e + 1],
+                scalar2=0.0,
+                op0=ALU.mult,
+                op1=ALU.max,
             )
+
+        silu_codes = const.tile([P, P], U32, align_bytes=64)
+        silu_scales = const.tile([P, P], U8, align_bytes=64)
         bases_codes = const.tile([P, SPLINE_PASSES, P], U32, align_bytes=64)
         bases_scales = const.tile([P, SPLINE_PASSES, P], U8, align_bytes=64)
 
-        nc.vector.quantize_mx(
-            out=silu_codes[:].bitcast(FP8X4),
-            scales=silu_scales[:],
-            in_=silu_grouped[:].rearrange("p n t -> p (n t)"),
-        )
-        nc.vector.quantize_mx(
-            out=bases_codes[:].rearrange("p g n -> p (g n)").bitcast(FP8X4),
-            scales=bases_scales[:].rearrange("p g n -> p (g n)"),
-            in_=bases_grouped[:].rearrange("p g n t -> p (g n t)"),
-        )
+        def quantise_tokens():
+            nc.vector.quantize_mx(
+                out=silu_codes[:].bitcast(FP8X4),
+                scales=silu_scales[:],
+                in_=silu_grouped[:].rearrange("p n t -> p (n t)"),
+            )
+            nc.vector.quantize_mx(
+                out=bases_codes[:].rearrange("p g n -> p (g n)").bitcast(FP8X4),
+                scales=bases_scales[:].rearrange("p g n -> p (g n)"),
+                in_=bases_grouped[:].rearrange("p g n t -> p (g n t)"),
+            )
 
-        for r in range(ROUNDS):
+        quantised = []
+
+        def prepare(r):
+            spline_words = spline_rows[r][:].bitcast(F32)
+            spline_bank = []
+            for a in range(ROWS):
+                bank = banks.tile([P, BLOCKS, P], F32, tag="bank")
+                for j in range(BLOCKS):
+                    w = a * BLOCKS + j
+                    nc.tensor.transpose(bank[:, j, :], spline_words[:, w * P : (w + 1) * P], ident_f32[:])
+                spline_bank.append(bank)
             base_words = base_rows[r][:].bitcast(F32)
             base_bank = banks.tile([P, ROWS, HALVES, P], F32, tag="bank")
             for a in range(ROWS):
                 for u in range(HALVES):
                     w = a * HALVES + u
                     nc.tensor.transpose(base_bank[:, a, u, :], base_words[:, w * P : (w + 1) * P], ident_f32[:])
-            spline_words = spline_rows[r][:].bitcast(F32)
-            spline_bank = []
-            for a in range(ROWS):
-                bank = banks.tile([P, SPLINE_PASSES * HALVES, P], F32, tag="bank")
-                for j in range(SPLINE_PASSES * HALVES):
-                    w = a * SPLINE_PASSES * HALVES + j
-                    nc.tensor.transpose(bank[:, j, :], spline_words[:, w * P : (w + 1) * P], ident_f32[:])
-                spline_bank.append(bank)
 
-            base_grouped = work.tile([P, F_ROUND, PACK], BF16, align_bytes=64)
+            spline_grouped = work.tile([P, SPLINE_PASSES, F_ROUND, PACK], BF16, align_bytes=64)
+            spline_grouped_words = spline_grouped[:].bitcast(F32)
+            nc.scalar.copy(
+                out=spline_grouped_words[:, :, 0:P, :],
+                in_=spline_bank[0][:].rearrange("p (g u) f -> p g f u", u=HALVES),
+            )
             nc.vector.tensor_copy(
+                out=spline_grouped_words[:, :, P : 2 * P, :],
+                in_=spline_bank[1][:].rearrange("p (g u) f -> p g f u", u=HALVES),
+            )
+            base_grouped = work.tile([P, F_ROUND, PACK], BF16, align_bytes=64)
+            nc.scalar.copy(
                 out=base_grouped[:].bitcast(F32).rearrange("p (a f) u -> p a f u", a=ROWS),
                 in_=base_bank[:].rearrange("p a u f -> p a f u"),
             )
-            spline_grouped = work.tile([P, SPLINE_PASSES, F_ROUND, PACK], BF16, align_bytes=64)
-            for a in range(ROWS):
-                nc.scalar.copy(
-                    out=spline_grouped[:].bitcast(F32)[:, :, a * P : (a + 1) * P, :],
-                    in_=spline_bank[a][:].rearrange("p (g u) f -> p g f u", u=HALVES),
-                )
 
-            base_codes = work.tile([P, F_ROUND], U32, align_bytes=64)
-            base_scales = work.tile([P, F_ROUND], U8, align_bytes=64)
-            nc.vector.quantize_mx(
-                out=base_codes[:].bitcast(FP8X4),
-                scales=base_scales[:],
-                in_=base_grouped[:].rearrange("p f t -> p (f t)"),
-            )
-            idle_passes(KEEP_PASSES, base_codes, base_scales)
-            spline_codes = work.tile([P, SPLINE_PASSES, F_ROUND], U32, align_bytes=64)
-            spline_scales = work.tile([P, SPLINE_PASSES, F_ROUND], U8, align_bytes=64)
+            spline_codes = resident.tile([P, SPLINE_PASSES, F_ROUND], U32, align_bytes=64)
+            spline_scales = resident.tile([P, SPLINE_PASSES, F_ROUND], U8, align_bytes=64)
             nc.vector.quantize_mx(
                 out=spline_codes[:].rearrange("p g f -> p (g f)").bitcast(FP8X4),
                 scales=spline_scales[:].rearrange("p g f -> p (g f)"),
                 in_=spline_grouped[:].rearrange("p g f t -> p (g f t)"),
             )
-
-            product = product_banks.tile([P, BANK], F32)
-            nc.tensor.matmul_mx(
-                out=product[:, :F_ROUND],
-                lhsT=silu_codes[:].bitcast(FP8X4),
-                lhsT_scale=silu_scales[:],
-                rhs=base_codes[:].bitcast(FP8X4),
-                rhs_scale=base_scales[:],
-                start=True,
-                stop=False,
+            base_codes = resident.tile([P, F_ROUND], U32, align_bytes=64)
+            base_scales = resident.tile([P, F_ROUND], U8, align_bytes=64)
+            nc.vector.quantize_mx(
+                out=base_codes[:].bitcast(FP8X4),
+                scales=base_scales[:],
+                in_=base_grouped[:].rearrange("p f t -> p (f t)"),
             )
+            quantised.append((spline_codes, spline_scales, base_codes, base_scales))
+
+        def multiply(r):
+            spline_codes, spline_scales, base_codes, base_scales = quantised[r]
+            product = product_banks.tile([P, BANK], F32, tag="product")
             for g in range(SPLINE_PASSES):
                 nc.tensor.matmul_mx(
                     out=product[:, :F_ROUND],
@@ -214,13 +203,30 @@ def tile_kanblock_pa_s_kernel(tc, x, grid, w1_base, w1_spline, out):
                     lhsT_scale=bases_scales[:, g, :],
                     rhs=spline_codes[:, g, :].bitcast(FP8X4),
                     rhs_scale=spline_scales[:, g, :],
-                    start=False,
-                    stop=(g == SPLINE_PASSES - 1),
+                    start=(g == 0),
+                    stop=False,
                 )
-
+            nc.tensor.matmul_mx(
+                out=product[:, :F_ROUND],
+                lhsT=silu_codes[:].bitcast(FP8X4),
+                lhsT_scale=silu_scales[:],
+                rhs=base_codes[:].bitcast(FP8X4),
+                rhs_scale=base_scales[:],
+                start=False,
+                stop=True,
+            )
             result = work.tile([P, F_ROUND], F32)
             nc.scalar.copy(
                 out=result[:].rearrange("n (f a) -> n f a", a=ROWS),
                 in_=product[:, :F_ROUND].rearrange("n (a f) -> n f a", a=ROWS),
             )
             nc.sync.dma_start(out=out[:, r * F_ROUND : (r + 1) * F_ROUND], in_=result[:])
+
+        prepare(0)
+        quantise_tokens()
+        for r in range(1, LAG):
+            prepare(r)
+        for r in range(ROUNDS):
+            if r + LAG < ROUNDS:
+                prepare(r + LAG)
+            multiply(r)

@@ -7,6 +7,7 @@ BF16 = mybir.dt.bfloat16
 F32 = mybir.dt.float32
 U32 = mybir.dt.uint32
 U8 = mybir.dt.uint8
+I32 = mybir.dt.int32
 FP8X4 = mybir.dt.float8_e4m3fn_x4
 ACT = mybir.ActivationFunctionType
 ALU = mybir.AluOpType
@@ -24,6 +25,8 @@ F_ROUND = ROWS * P
 ROUNDS = F // F_ROUND
 LAG = 2
 BANK = 512
+WARM_PASSES = 8
+KEEP_PASSES = 4
 
 FLOPS = 2 * P * F * (D + D * BASES)
 
@@ -39,8 +42,9 @@ def tile_kanblock_pa_s_kernel(tc, x, grid, w1_base, w1_spline, out):
         const = stack.enter_context(tc.tile_pool(name="const", bufs=1))
         resident = stack.enter_context(tc.tile_pool(name="resident", bufs=ROUNDS))
         work = stack.enter_context(tc.tile_pool(name="work", bufs=2))
-        banks = stack.enter_context(tc.psum_pool(name="banks", bufs=6))
+        banks = stack.enter_context(tc.psum_pool(name="banks", bufs=5))
         product_banks = stack.enter_context(tc.psum_pool(name="product_banks", bufs=2))
+        idle_banks = stack.enter_context(tc.psum_pool(name="idle_banks", bufs=1))
 
         knots_bf = const.tile([P, 4], BF16)
         nc.scalar.dma_start(out=knots_bf[:], in_=grid.partition_broadcast(P))
@@ -55,6 +59,27 @@ def tile_kanblock_pa_s_kernel(tc, x, grid, w1_base, w1_spline, out):
             base_sb = resident.tile([P, ROWS * D], BF16)
             nc.sync.dma_start(out=base_sb[:], in_=base_rounds[r])
             base_rows.append(base_sb)
+
+        idle_bank = idle_banks.tile([P, BANK], F32)
+        zeros = const.tile([P, F_ROUND * PACK], BF16, align_bytes=64)
+        nc.vector.memset(zeros[:].bitcast(I32), 0)
+        zero_codes = const.tile([P, F_ROUND], U32, align_bytes=64)
+        zero_scales = const.tile([P, F_ROUND], U8, align_bytes=64)
+        nc.vector.quantize_mx(out=zero_codes[:].bitcast(FP8X4), scales=zero_scales[:], in_=zeros[:])
+
+        def idle_passes(count):
+            for i in range(count):
+                nc.tensor.matmul_mx(
+                    out=idle_bank[:, :F_ROUND],
+                    lhsT=zero_codes[:, :P].bitcast(FP8X4),
+                    lhsT_scale=zero_scales[:, :P],
+                    rhs=zero_codes[:].bitcast(FP8X4),
+                    rhs_scale=zero_scales[:],
+                    start=True,
+                    stop=True,
+                )
+
+        idle_passes(WARM_PASSES)
 
         warm = const.tile([P, 1], F32)
         nc.vector.memset(warm[:], 0.0)
@@ -160,6 +185,8 @@ def tile_kanblock_pa_s_kernel(tc, x, grid, w1_base, w1_spline, out):
                 for u in range(HALVES):
                     w = a * HALVES + u
                     nc.tensor.transpose(base_bank[:, a, u, :], base_words[:, w * P : (w + 1) * P], ident_f32[:])
+            if r < ROUNDS - 1:
+                idle_passes(KEEP_PASSES)
 
             spline_grouped = work.tile([P, SPLINE_PASSES, F_ROUND, PACK], BF16, align_bytes=64)
             spline_grouped_words = spline_grouped[:].bitcast(F32)

@@ -7,7 +7,6 @@ BF16 = mybir.dt.bfloat16
 F32 = mybir.dt.float32
 U32 = mybir.dt.uint32
 U8 = mybir.dt.uint8
-I32 = mybir.dt.int32
 FP8X4 = mybir.dt.float8_e4m3fn_x4
 ACT = mybir.ActivationFunctionType
 ALU = mybir.AluOpType
@@ -25,8 +24,6 @@ F_ROUND = ROWS * P
 ROUNDS = F // F_ROUND
 LAG = 2
 BANK = 512
-WARM_PASSES = 8
-KEEP_PASSES = 4
 
 FLOPS = 2 * P * F * (D + D * BASES)
 
@@ -42,9 +39,7 @@ def tile_kanblock_pa_s_kernel(tc, x, grid, w1_base, w1_spline, out):
         const = stack.enter_context(tc.tile_pool(name="const", bufs=1))
         resident = stack.enter_context(tc.tile_pool(name="resident", bufs=ROUNDS))
         work = stack.enter_context(tc.tile_pool(name="work", bufs=2))
-        banks = stack.enter_context(tc.psum_pool(name="banks", bufs=5))
-        product_banks = stack.enter_context(tc.psum_pool(name="product_banks", bufs=2))
-        idle_banks = stack.enter_context(tc.psum_pool(name="idle_banks", bufs=1))
+        banks = stack.enter_context(tc.psum_pool(name="banks", bufs=8))
 
         knots_bf = const.tile([P, 4], BF16)
         nc.scalar.dma_start(out=knots_bf[:], in_=grid.partition_broadcast(P))
@@ -60,27 +55,6 @@ def tile_kanblock_pa_s_kernel(tc, x, grid, w1_base, w1_spline, out):
             nc.sync.dma_start(out=base_sb[:], in_=base_rounds[r])
             base_rows.append(base_sb)
 
-        idle_bank = idle_banks.tile([P, BANK], F32)
-        zeros = const.tile([P, F_ROUND * PACK], BF16, align_bytes=64)
-        nc.vector.memset(zeros[:].bitcast(I32), 0)
-        zero_codes = const.tile([P, F_ROUND], U32, align_bytes=64)
-        zero_scales = const.tile([P, F_ROUND], U8, align_bytes=64)
-        nc.vector.quantize_mx(out=zero_codes[:].bitcast(FP8X4), scales=zero_scales[:], in_=zeros[:])
-
-        def idle_passes(count):
-            for i in range(count):
-                nc.tensor.matmul_mx(
-                    out=idle_bank[:, :F_ROUND],
-                    lhsT=zero_codes[:, :P].bitcast(FP8X4),
-                    lhsT_scale=zero_scales[:, :P],
-                    rhs=zero_codes[:].bitcast(FP8X4),
-                    rhs_scale=zero_scales[:],
-                    start=True,
-                    stop=True,
-                )
-
-        idle_passes(WARM_PASSES)
-
         warm = const.tile([P, 1], F32)
         nc.vector.memset(warm[:], 0.0)
         nc.scalar.activation(out=warm[:], in_=warm[:], func=ACT.Silu)
@@ -95,60 +69,58 @@ def tile_kanblock_pa_s_kernel(tc, x, grid, w1_base, w1_spline, out):
         nc.vector.tensor_sub(out=width[:], in0=knots[:, 1:4], in1=knots[:, 0:3])
         slope = const.tile([P, 3], F32)
         nc.vector.reciprocal(out=slope[:], in_=width[:])
-        ratio = const.tile([P, BASES], F32)
-        nc.vector.scalar_tensor_tensor(
-            out=ratio[:], in0=slope[:, 1:3], scalar=-1.0, in1=width[:, 0:2], op0=ALU.mult, op1=ALU.mult
-        )
-        shift = const.tile([P, BASES], F32)
-        nc.vector.scalar_tensor_tensor(
-            out=shift[:], in0=knots[:, 2:4], scalar=-1.0, in1=ratio[:], op0=ALU.mult, op1=ALU.mult
-        )
+        fall_slope = const.tile([P, BASES], F32)
+        nc.vector.tensor_scalar_mul(out=fall_slope[:], in0=slope[:, 1:3], scalar1=-1.0)
+        fall_shift = const.tile([P, BASES], F32)
+        nc.vector.tensor_mul(out=fall_shift[:], in0=slope[:, 1:3], in1=knots[:, 2:4])
 
-        x_words = product_banks.tile([P, HALVES, P], F32, tag="product")
-        x_feat_vector = product_banks.tile([P, BLOCKS, P], BF16, tag="product")
         x_feat_scalar = banks.tile([P, BLOCKS, P], BF16, tag="bank")
+        x_feat_vector = banks.tile([P, BLOCKS, P], BF16, tag="bank")
         for x_feat in (x_feat_scalar, x_feat_vector):
             for j in range(BLOCKS):
                 nc.tensor.transpose(x_feat[:, j, :], x_sb[:, j * P : (j + 1) * P], ident_bf16[:])
+        x_words = banks.tile([P, HALVES, P], F32, tag="bank")
         for u in range(HALVES):
             nc.tensor.transpose(x_words[:, u, :], x_sb[:].bitcast(F32)[:, u * P : (u + 1) * P], ident_f32[:])
 
-        bases_grouped = const.tile([P, SPLINE_PASSES, P, PACK], BF16, align_bytes=64)
-        bases_by_e = bases_grouped[:].rearrange("p g n (u e) -> p e g n u", e=BASES)
+        rising = []
         falling = []
         for e in range(BASES):
-            line = work.tile([P, BLOCKS, P], F32)
-            nc.scalar.activation(
-                out=line[:],
-                in_=x_feat_scalar[:],
-                func=ACT.Identity,
-                scale=ratio[:, e : e + 1],
-                bias=shift[:, e : e + 1],
+            rise = work.tile([P, SPLINE_PASSES, P, HALVES], F32)
+            nc.vector.tensor_scalar(
+                out=rise[:],
+                in0=x_feat_vector[:].rearrange("p (g u) n -> p g n u", u=HALVES),
+                scalar1=knots[:, e : e + 1],
+                scalar2=slope[:, e : e + 1],
+                op0=ALU.subtract,
+                op1=ALU.mult,
             )
-            falling.append(line)
+            rising.append(rise)
+            fall = work.tile([P, SPLINE_PASSES, P, HALVES], F32)
+            nc.scalar.activation(
+                out=fall[:],
+                in_=x_feat_scalar[:].rearrange("p (g u) n -> p g n u", u=HALVES),
+                func=ACT.Relu,
+                scale=fall_slope[:, e : e + 1],
+                bias=fall_shift[:, e : e + 1],
+            )
+            falling.append(fall)
         silu_grouped = const.tile([P, P, PACK], BF16, align_bytes=64)
         nc.scalar.activation(
             out=silu_grouped[:].rearrange("p n (u e) -> p n u e", e=2),
             in_=x_words[:].bitcast(BF16).rearrange("p u (n e) -> p n u e", e=2),
             func=ACT.Silu,
         )
+        bases_grouped = const.tile([P, SPLINE_PASSES, P, PACK], BF16, align_bytes=64)
+        bases_by_e = bases_grouped[:].rearrange("p g n (u e) -> p e (g n u)", e=BASES)
         for e in range(BASES):
-            tent = work.tile([P, BLOCKS, P], F32)
             nc.vector.scalar_tensor_tensor(
-                out=tent[:],
-                in0=x_feat_vector[:],
-                scalar=knots[:, e : e + 1],
-                in1=falling[e][:],
-                op0=ALU.subtract,
-                op1=ALU.min,
-            )
-            nc.vector.tensor_scalar(
                 out=bases_by_e[:, e],
-                in0=tent[:].rearrange("p (g u) n -> p g n u", u=HALVES),
-                scalar1=slope[:, e : e + 1],
-                scalar2=0.0,
-                op0=ALU.mult,
-                op1=ALU.max,
+                in0=rising[e][:].rearrange("p g n u -> p (g n u)"),
+                scalar=0.0,
+                in1=falling[e][:].rearrange("p g n u -> p (g n u)"),
+                op0=ALU.max,
+                op1=ALU.min,
             )
 
         silu_codes = const.tile([P, P], U32, align_bytes=64)
@@ -185,20 +157,15 @@ def tile_kanblock_pa_s_kernel(tc, x, grid, w1_base, w1_spline, out):
                 for u in range(HALVES):
                     w = a * HALVES + u
                     nc.tensor.transpose(base_bank[:, a, u, :], base_words[:, w * P : (w + 1) * P], ident_f32[:])
-            if r < ROUNDS - 1:
-                idle_passes(KEEP_PASSES)
 
-            spline_grouped = work.tile([P, SPLINE_PASSES, F_ROUND, PACK], BF16, align_bytes=64)
+            spline_grouped = resident.tile([P, SPLINE_PASSES, F_ROUND, PACK], BF16, align_bytes=64)
             spline_grouped_words = spline_grouped[:].bitcast(F32)
-            nc.scalar.copy(
-                out=spline_grouped_words[:, :, 0:P, :],
-                in_=spline_bank[0][:].rearrange("p (g u) f -> p g f u", u=HALVES),
-            )
-            nc.vector.tensor_copy(
-                out=spline_grouped_words[:, :, P : 2 * P, :],
-                in_=spline_bank[1][:].rearrange("p (g u) f -> p g f u", u=HALVES),
-            )
-            base_grouped = work.tile([P, F_ROUND, PACK], BF16, align_bytes=64)
+            for a in range(ROWS):
+                nc.scalar.copy(
+                    out=spline_grouped_words[:, :, a * P : (a + 1) * P, :],
+                    in_=spline_bank[a][:].rearrange("p (g u) f -> p g f u", u=HALVES),
+                )
+            base_grouped = resident.tile([P, F_ROUND, PACK], BF16, align_bytes=64)
             nc.scalar.copy(
                 out=base_grouped[:].bitcast(F32).rearrange("p (a f) u -> p a f u", a=ROWS),
                 in_=base_bank[:].rearrange("p a u f -> p a f u"),
@@ -222,7 +189,7 @@ def tile_kanblock_pa_s_kernel(tc, x, grid, w1_base, w1_spline, out):
 
         def multiply(r):
             spline_codes, spline_scales, base_codes, base_scales = quantised[r]
-            product = product_banks.tile([P, BANK], F32, tag="product")
+            product = banks.tile([P, BANK], F32, tag="bank")
             for g in range(SPLINE_PASSES):
                 nc.tensor.matmul_mx(
                     out=product[:, :F_ROUND],
@@ -242,11 +209,13 @@ def tile_kanblock_pa_s_kernel(tc, x, grid, w1_base, w1_spline, out):
                 start=False,
                 stop=True,
             )
-            result = work.tile([P, F_ROUND], F32)
-            nc.scalar.copy(
-                out=result[:].rearrange("n (f a) -> n f a", a=ROWS),
-                in_=product[:, :F_ROUND].rearrange("n (a f) -> n f a", a=ROWS),
-            )
+            result = resident.tile([P, F_ROUND], F32)
+            result_columns = result[:].rearrange("n (f a) -> n f a", a=ROWS)
+            product_columns = product[:, :F_ROUND].rearrange("n (a f) -> n f a", a=ROWS)
+            if r % 2 == 0:
+                nc.vector.tensor_copy(out=result_columns, in_=product_columns)
+            else:
+                nc.scalar.copy(out=result_columns, in_=product_columns)
             nc.sync.dma_start(out=out[:, r * F_ROUND : (r + 1) * F_ROUND], in_=result[:])
 
         prepare(0)

@@ -19,10 +19,9 @@ BASES = 2
 SPLINE_PASSES = D * BASES // (P * PACK)
 BLOCKS = D // P
 F = 1024
-ROWS = 2
-F_ROUND = ROWS * P
-ROUNDS = F // F_ROUND
-LAG = 2
+ROUND_ROWS = (2, 2, 2, 1, 1)
+ROUNDS = len(ROUND_ROWS)
+LAG = 3
 BANK = 512
 
 FLOPS = 2 * P * F * (D + D * BASES)
@@ -31,8 +30,8 @@ FLOPS = 2 * P * F * (D + D * BASES)
 def tile_kanblock_pa_s_kernel(tc, x, grid, w1_base, w1_spline, out):
     nc = tc.nc
     x_rows = x.flatten_outer_dims()
-    base_rounds = w1_base.rearrange("(r p a) k -> r p (a k)", p=P, a=ROWS)
-    spline_rounds = w1_spline.rearrange("(r p a) i g -> r p (a i g)", p=P, a=ROWS)
+    assert sum(ROUND_ROWS) * P == F
+    first_row = [P * sum(ROUND_ROWS[:r]) for r in range(ROUNDS)]
 
     with ExitStack() as stack:
         stack.enter_context(tc.manual_schedule())
@@ -48,11 +47,13 @@ def tile_kanblock_pa_s_kernel(tc, x, grid, w1_base, w1_spline, out):
         base_rows = []
         spline_rows = []
         for r in range(ROUNDS):
-            spline_sb = resident.tile([P, ROWS * D * BASES], BF16)
-            nc.sync.dma_start(out=spline_sb[:], in_=spline_rounds[r])
+            rows = ROUND_ROWS[r]
+            these = slice(first_row[r], first_row[r] + rows * P)
+            spline_sb = resident.tile([P, rows * D * BASES], BF16)
+            nc.sync.dma_start(out=spline_sb[:], in_=w1_spline[these].rearrange("(p a) i g -> p (a i g)", a=rows))
             spline_rows.append(spline_sb)
-            base_sb = resident.tile([P, ROWS * D], BF16)
-            nc.sync.dma_start(out=base_sb[:], in_=base_rounds[r])
+            base_sb = resident.tile([P, rows * D], BF16)
+            nc.sync.dma_start(out=base_sb[:], in_=w1_base[these].rearrange("(p a) k -> p (a k)", a=rows))
             base_rows.append(base_sb)
 
         warm = const.tile([P, 1], F32)
@@ -69,58 +70,59 @@ def tile_kanblock_pa_s_kernel(tc, x, grid, w1_base, w1_spline, out):
         nc.vector.tensor_sub(out=width[:], in0=knots[:, 1:4], in1=knots[:, 0:3])
         slope = const.tile([P, 3], F32)
         nc.vector.reciprocal(out=slope[:], in_=width[:])
-        fall_slope = const.tile([P, BASES], F32)
-        nc.vector.tensor_scalar_mul(out=fall_slope[:], in0=slope[:, 1:3], scalar1=-1.0)
-        fall_shift = const.tile([P, BASES], F32)
-        nc.vector.tensor_mul(out=fall_shift[:], in0=slope[:, 1:3], in1=knots[:, 2:4])
+        ratio = const.tile([P, BASES], F32)
+        nc.vector.scalar_tensor_tensor(
+            out=ratio[:], in0=slope[:, 1:3], scalar=-1.0, in1=width[:, 0:2], op0=ALU.mult, op1=ALU.mult
+        )
 
-        x_feat_scalar = banks.tile([P, BLOCKS, P], BF16, tag="bank")
-        x_feat_vector = banks.tile([P, BLOCKS, P], BF16, tag="bank")
-        for x_feat in (x_feat_scalar, x_feat_vector):
-            for j in range(BLOCKS):
-                nc.tensor.transpose(x_feat[:, j, :], x_sb[:, j * P : (j + 1) * P], ident_bf16[:])
+        x_feat = banks.tile([P, BLOCKS, P], BF16, tag="bank")
+        for j in range(BLOCKS):
+            nc.tensor.transpose(x_feat[:, j, :], x_sb[:, j * P : (j + 1) * P], ident_bf16[:])
         x_words = banks.tile([P, HALVES, P], F32, tag="bank")
         for u in range(HALVES):
             nc.tensor.transpose(x_words[:, u, :], x_sb[:].bitcast(F32)[:, u * P : (u + 1) * P], ident_f32[:])
 
-        rising = []
-        falling = []
-        for e in range(BASES):
-            rise = work.tile([P, SPLINE_PASSES, P, HALVES], F32)
-            nc.vector.tensor_scalar(
-                out=rise[:],
-                in0=x_feat_vector[:].rearrange("p (g u) n -> p g n u", u=HALVES),
-                scalar1=knots[:, e : e + 1],
-                scalar2=slope[:, e : e + 1],
-                op0=ALU.subtract,
-                op1=ALU.mult,
-            )
-            rising.append(rise)
-            fall = work.tile([P, SPLINE_PASSES, P, HALVES], F32)
-            nc.scalar.activation(
-                out=fall[:],
-                in_=x_feat_scalar[:].rearrange("p (g u) n -> p g n u", u=HALVES),
-                func=ACT.Relu,
-                scale=fall_slope[:, e : e + 1],
-                bias=fall_shift[:, e : e + 1],
-            )
-            falling.append(fall)
         silu_grouped = const.tile([P, P, PACK], BF16, align_bytes=64)
         nc.scalar.activation(
             out=silu_grouped[:].rearrange("p n (u e) -> p n u e", e=2),
             in_=x_words[:].bitcast(BF16).rearrange("p u (n e) -> p n u e", e=2),
             func=ACT.Silu,
         )
-        bases_grouped = const.tile([P, SPLINE_PASSES, P, PACK], BF16, align_bytes=64)
-        bases_by_e = bases_grouped[:].rearrange("p g n (u e) -> p e (g n u)", e=BASES)
+
+        falling = []
         for e in range(BASES):
+            fall = work.tile([P, BLOCKS, P], F32)
+            nc.vector.tensor_scalar(
+                out=fall[:],
+                in0=x_feat[:],
+                scalar1=knots[:, e + 2 : e + 3],
+                scalar2=ratio[:, e : e + 1],
+                op0=ALU.subtract,
+                op1=ALU.mult,
+            )
+            falling.append(fall)
+        tents = []
+        for e in range(BASES):
+            tent = work.tile([P, BLOCKS, P], F32)
             nc.vector.scalar_tensor_tensor(
-                out=bases_by_e[:, e],
-                in0=rising[e][:].rearrange("p g n u -> p (g n u)"),
-                scalar=0.0,
-                in1=falling[e][:].rearrange("p g n u -> p (g n u)"),
-                op0=ALU.max,
+                out=tent[:],
+                in0=x_feat[:],
+                scalar=knots[:, e : e + 1],
+                in1=falling[e][:],
+                op0=ALU.subtract,
                 op1=ALU.min,
+            )
+            tents.append(tent)
+        bases_grouped = const.tile([P, SPLINE_PASSES, P, PACK], BF16, align_bytes=64)
+        bases_by_e = bases_grouped[:].rearrange("p g n (u e) -> p e g n u", e=BASES)
+        for e in range(BASES):
+            nc.vector.tensor_scalar(
+                out=bases_by_e[:, e],
+                in0=tents[e][:].rearrange("p (g u) n -> p g n u", u=HALVES),
+                scalar1=slope[:, e : e + 1],
+                scalar2=0.0,
+                op0=ALU.mult,
+                op1=ALU.max,
             )
 
         silu_codes = const.tile([P, P], U32, align_bytes=64)
@@ -143,43 +145,45 @@ def tile_kanblock_pa_s_kernel(tc, x, grid, w1_base, w1_spline, out):
         quantised = []
 
         def prepare(r):
+            rows = ROUND_ROWS[r]
+            columns = rows * P
             spline_words = spline_rows[r][:].bitcast(F32)
             spline_bank = []
-            for a in range(ROWS):
+            for a in range(rows):
                 bank = banks.tile([P, BLOCKS, P], F32, tag="bank")
                 for j in range(BLOCKS):
                     w = a * BLOCKS + j
                     nc.tensor.transpose(bank[:, j, :], spline_words[:, w * P : (w + 1) * P], ident_f32[:])
                 spline_bank.append(bank)
             base_words = base_rows[r][:].bitcast(F32)
-            base_bank = banks.tile([P, ROWS, HALVES, P], F32, tag="bank")
-            for a in range(ROWS):
+            base_bank = banks.tile([P, rows, HALVES, P], F32, tag="bank")
+            for a in range(rows):
                 for u in range(HALVES):
                     w = a * HALVES + u
                     nc.tensor.transpose(base_bank[:, a, u, :], base_words[:, w * P : (w + 1) * P], ident_f32[:])
 
-            spline_grouped = resident.tile([P, SPLINE_PASSES, F_ROUND, PACK], BF16, align_bytes=64)
+            spline_grouped = resident.tile([P, SPLINE_PASSES, columns, PACK], BF16, align_bytes=64)
             spline_grouped_words = spline_grouped[:].bitcast(F32)
-            for a in range(ROWS):
+            for a in range(rows):
                 nc.scalar.copy(
                     out=spline_grouped_words[:, :, a * P : (a + 1) * P, :],
                     in_=spline_bank[a][:].rearrange("p (g u) f -> p g f u", u=HALVES),
                 )
-            base_grouped = resident.tile([P, F_ROUND, PACK], BF16, align_bytes=64)
+            base_grouped = resident.tile([P, columns, PACK], BF16, align_bytes=64)
             nc.scalar.copy(
-                out=base_grouped[:].bitcast(F32).rearrange("p (a f) u -> p a f u", a=ROWS),
+                out=base_grouped[:].bitcast(F32).rearrange("p (a f) u -> p a f u", a=rows),
                 in_=base_bank[:].rearrange("p a u f -> p a f u"),
             )
 
-            spline_codes = resident.tile([P, SPLINE_PASSES, F_ROUND], U32, align_bytes=64)
-            spline_scales = resident.tile([P, SPLINE_PASSES, F_ROUND], U8, align_bytes=64)
+            spline_codes = resident.tile([P, SPLINE_PASSES, columns], U32, align_bytes=64)
+            spline_scales = resident.tile([P, SPLINE_PASSES, columns], U8, align_bytes=64)
             nc.vector.quantize_mx(
                 out=spline_codes[:].rearrange("p g f -> p (g f)").bitcast(FP8X4),
                 scales=spline_scales[:].rearrange("p g f -> p (g f)"),
                 in_=spline_grouped[:].rearrange("p g f t -> p (g f t)"),
             )
-            base_codes = resident.tile([P, F_ROUND], U32, align_bytes=64)
-            base_scales = resident.tile([P, F_ROUND], U8, align_bytes=64)
+            base_codes = resident.tile([P, columns], U32, align_bytes=64)
+            base_scales = resident.tile([P, columns], U8, align_bytes=64)
             nc.vector.quantize_mx(
                 out=base_codes[:].bitcast(FP8X4),
                 scales=base_scales[:],
@@ -189,10 +193,12 @@ def tile_kanblock_pa_s_kernel(tc, x, grid, w1_base, w1_spline, out):
 
         def multiply(r):
             spline_codes, spline_scales, base_codes, base_scales = quantised[r]
+            rows = ROUND_ROWS[r]
+            columns = rows * P
             product = banks.tile([P, BANK], F32, tag="bank")
             for g in range(SPLINE_PASSES):
                 nc.tensor.matmul_mx(
-                    out=product[:, :F_ROUND],
+                    out=product[:, :columns],
                     lhsT=bases_codes[:, g, :].bitcast(FP8X4),
                     lhsT_scale=bases_scales[:, g, :],
                     rhs=spline_codes[:, g, :].bitcast(FP8X4),
@@ -201,7 +207,7 @@ def tile_kanblock_pa_s_kernel(tc, x, grid, w1_base, w1_spline, out):
                     stop=False,
                 )
             nc.tensor.matmul_mx(
-                out=product[:, :F_ROUND],
+                out=product[:, :columns],
                 lhsT=silu_codes[:].bitcast(FP8X4),
                 lhsT_scale=silu_scales[:],
                 rhs=base_codes[:].bitcast(FP8X4),
@@ -209,14 +215,14 @@ def tile_kanblock_pa_s_kernel(tc, x, grid, w1_base, w1_spline, out):
                 start=False,
                 stop=True,
             )
-            result = resident.tile([P, F_ROUND], F32)
-            result_columns = result[:].rearrange("n (f a) -> n f a", a=ROWS)
-            product_columns = product[:, :F_ROUND].rearrange("n (a f) -> n f a", a=ROWS)
+            result = resident.tile([P, columns], F32)
+            result_columns = result[:].rearrange("n (f a) -> n f a", a=rows)
+            product_columns = product[:, :columns].rearrange("n (a f) -> n f a", a=rows)
             if r % 2 == 0:
                 nc.vector.tensor_copy(out=result_columns, in_=product_columns)
             else:
                 nc.scalar.copy(out=result_columns, in_=product_columns)
-            nc.sync.dma_start(out=out[:, r * F_ROUND : (r + 1) * F_ROUND], in_=result[:])
+            nc.sync.dma_start(out=out[:, first_row[r] : first_row[r] + columns], in_=result[:])
 
         prepare(0)
         quantise_tokens()

@@ -37,7 +37,6 @@ def tile_kanblock_pa_s_kernel(tc, x, grid, w1_base, w1_spline, out):
         stack.enter_context(tc.manual_schedule())
         const = stack.enter_context(tc.tile_pool(name="const", bufs=1))
         resident = stack.enter_context(tc.tile_pool(name="resident", bufs=ROUNDS))
-        work = stack.enter_context(tc.tile_pool(name="work", bufs=2))
         banks = stack.enter_context(tc.psum_pool(name="banks", bufs=8))
 
         knots_bf = const.tile([P, 4], BF16)
@@ -66,14 +65,11 @@ def tile_kanblock_pa_s_kernel(tc, x, grid, w1_base, w1_spline, out):
 
         knots = const.tile([P, 4], F32)
         nc.vector.tensor_copy(out=knots[:], in_=knots_bf[:])
-        width = const.tile([P, 3], F32)
-        nc.vector.tensor_sub(out=width[:], in0=knots[:, 1:4], in1=knots[:, 0:3])
-        slope = const.tile([P, 3], F32)
+        width = const.tile([P, 2, 3], F32)
+        nc.vector.tensor_sub(out=width[:, 0, :], in0=knots_bf[:, 1:4], in1=knots_bf[:, 0:3])
+        nc.vector.tensor_sub(out=width[:, 1, :], in0=knots_bf[:, 0:3], in1=knots_bf[:, 1:4])
+        slope = const.tile([P, 2, 3], F32)
         nc.vector.reciprocal(out=slope[:], in_=width[:])
-        ratio = const.tile([P, BASES], F32)
-        nc.vector.scalar_tensor_tensor(
-            out=ratio[:], in0=slope[:, 1:3], scalar=-1.0, in1=width[:, 0:2], op0=ALU.mult, op1=ALU.mult
-        )
 
         x_feat = banks.tile([P, BLOCKS, P], BF16, tag="bank")
         for j in range(BLOCKS):
@@ -89,41 +85,35 @@ def tile_kanblock_pa_s_kernel(tc, x, grid, w1_base, w1_spline, out):
             func=ACT.Silu,
         )
 
-        falling = []
-        for e in range(BASES):
-            fall = work.tile([P, BLOCKS, P], F32)
+        x_clamped = const.tile([P, SPLINE_PASSES, P, HALVES], BF16)
+        nc.vector.tensor_scalar(
+            out=x_clamped[:],
+            in0=x_feat[:].rearrange("p (g u) n -> p g n u", u=HALVES),
+            scalar1=knots[:, 0:1],
+            scalar2=knots[:, 3:4],
+            op0=ALU.max,
+            op1=ALU.min,
+        )
+        outer = const.tile([P, BASES, D], F32)
+        inner = const.tile([P, BASES, D], F32)
+        for line, e, knot, sign, m in ((inner, 0, 2, 1, 1), (inner, 1, 1, 0, 1), (outer, 0, 0, 0, 0), (outer, 1, 3, 1, 2)):
             nc.vector.tensor_scalar(
-                out=fall[:],
-                in0=x_feat[:],
-                scalar1=knots[:, e + 2 : e + 3],
-                scalar2=ratio[:, e : e + 1],
+                out=line[:, e, :],
+                in0=x_clamped[:].rearrange("p g n u -> p (g n u)"),
+                scalar1=knots[:, knot : knot + 1],
+                scalar2=slope[:, sign, m : m + 1],
                 op0=ALU.subtract,
                 op1=ALU.mult,
             )
-            falling.append(fall)
-        tents = []
-        for e in range(BASES):
-            tent = work.tile([P, BLOCKS, P], F32)
-            nc.vector.scalar_tensor_tensor(
-                out=tent[:],
-                in0=x_feat[:],
-                scalar=knots[:, e : e + 1],
-                in1=falling[e][:],
-                op0=ALU.subtract,
-                op1=ALU.min,
-            )
-            tents.append(tent)
         bases_grouped = const.tile([P, SPLINE_PASSES, P, PACK], BF16, align_bytes=64)
-        bases_by_e = bases_grouped[:].rearrange("p g n (u e) -> p e g n u", e=BASES)
-        for e in range(BASES):
-            nc.vector.tensor_scalar(
-                out=bases_by_e[:, e],
-                in0=tents[e][:].rearrange("p (g u) n -> p g n u", u=HALVES),
-                scalar1=slope[:, e : e + 1],
-                scalar2=0.0,
-                op0=ALU.mult,
-                op1=ALU.max,
-            )
+        nc.vector.scalar_tensor_tensor(
+            out=bases_grouped[:].rearrange("p g n (u e) -> p (g n u) e", e=BASES),
+            in0=inner[:].rearrange("p e c -> p c e"),
+            scalar=0.0,
+            in1=outer[:].rearrange("p e c -> p c e"),
+            op0=ALU.max,
+            op1=ALU.min,
+        )
 
         silu_codes = const.tile([P, P], U32, align_bytes=64)
         silu_scales = const.tile([P, P], U8, align_bytes=64)

@@ -39,8 +39,9 @@ def tile_kanblock_pa_s_kernel(tc, x, grid, w1_base, w1_spline, out):
         resident = stack.enter_context(tc.tile_pool(name="resident", bufs=ROUNDS))
         banks = stack.enter_context(tc.psum_pool(name="banks", bufs=8))
 
-        knots_bf = const.tile([P, 4], BF16)
-        nc.scalar.dma_start(out=knots_bf[:], in_=grid.partition_broadcast(P))
+        knots_row = const.tile([P, 4], BF16)
+        nc.vector.memset(knots_row[:], 0.0)
+        nc.scalar.dma_start(out=knots_row[0:1, :], in_=grid.rearrange("(o k) -> o k", o=1))
         x_sb = const.tile([P, D], BF16)
         nc.sync.dma_start(out=x_sb[:], in_=x_rows)
         base_rows = []
@@ -63,11 +64,15 @@ def tile_kanblock_pa_s_kernel(tc, x, grid, w1_base, w1_spline, out):
         ident_f32 = const.tile([P, P], F32)
         make_identity(nc, ident_f32[:])
 
+        ones = const.tile([P, P], BF16)
+        nc.vector.memset(ones[:], 1.0)
+        knots_bank = banks.tile([P, 4], F32, tag="bank")
+        nc.tensor.matmul(knots_bank[:], lhsT=ones[:], rhs=knots_row[:], start=True, stop=True)
         knots = const.tile([P, 4], F32)
-        nc.vector.tensor_copy(out=knots[:], in_=knots_bf[:])
+        nc.vector.tensor_copy(out=knots[:], in_=knots_bank[:])
         width = const.tile([P, 2, 3], F32)
-        nc.vector.tensor_sub(out=width[:, 0, :], in0=knots_bf[:, 1:4], in1=knots_bf[:, 0:3])
-        nc.vector.tensor_sub(out=width[:, 1, :], in0=knots_bf[:, 0:3], in1=knots_bf[:, 1:4])
+        nc.vector.tensor_sub(out=width[:, 0, :], in0=knots[:, 1:4], in1=knots[:, 0:3])
+        nc.vector.tensor_sub(out=width[:, 1, :], in0=knots[:, 0:3], in1=knots[:, 1:4])
         slope = const.tile([P, 2, 3], F32)
         nc.vector.reciprocal(out=slope[:], in_=width[:])
 

@@ -23,6 +23,9 @@ ROUND_ROWS = (2, 2, 2, 1, 1)
 ROUNDS = len(ROUND_ROWS)
 LAG = 3
 BANK = 512
+IDLE_COLUMNS = 256
+HEAD_IDLE = 4
+ROUND_IDLE = (4, 4, 4, 0, 0)
 
 FLOPS = 2 * P * F * (D + D * BASES)
 
@@ -37,7 +40,8 @@ def tile_kanblock_pa_s_kernel(tc, x, grid, w1_base, w1_spline, out):
         stack.enter_context(tc.manual_schedule())
         const = stack.enter_context(tc.tile_pool(name="const", bufs=1))
         resident = stack.enter_context(tc.tile_pool(name="resident", bufs=ROUNDS))
-        banks = stack.enter_context(tc.psum_pool(name="banks", bufs=8))
+        banks = stack.enter_context(tc.psum_pool(name="banks", bufs=7))
+        idle = stack.enter_context(tc.psum_pool(name="idle", bufs=1))
 
         knots_row = const.tile([P, 4], BF16)
         nc.vector.memset(knots_row[:], 0.0)
@@ -63,6 +67,27 @@ def tile_kanblock_pa_s_kernel(tc, x, grid, w1_base, w1_spline, out):
         make_identity(nc, ident_bf16[:])
         ident_f32 = const.tile([P, P], F32)
         make_identity(nc, ident_f32[:])
+
+        zero_values = const.tile([P, IDLE_COLUMNS * PACK], BF16, align_bytes=64)
+        nc.vector.memset(zero_values[:], 0.0)
+        zero_codes = const.tile([P, IDLE_COLUMNS], U32, align_bytes=64)
+        zero_scales = const.tile([P, IDLE_COLUMNS], U8, align_bytes=64)
+        nc.vector.quantize_mx(out=zero_codes[:].bitcast(FP8X4), scales=zero_scales[:], in_=zero_values[:])
+        idle_bank = idle.tile([P, IDLE_COLUMNS], F32)
+
+        def idle_passes(count):
+            for i in range(count):
+                nc.tensor.matmul_mx(
+                    out=idle_bank[:],
+                    lhsT=zero_codes[:, :P].bitcast(FP8X4),
+                    lhsT_scale=zero_scales[:, :P],
+                    rhs=zero_codes[:].bitcast(FP8X4),
+                    rhs_scale=zero_scales[:],
+                    start=True,
+                    stop=True,
+                )
+
+        idle_passes(HEAD_IDLE)
 
         ones = const.tile([P, P], BF16)
         nc.vector.memset(ones[:], 1.0)
@@ -150,6 +175,7 @@ def tile_kanblock_pa_s_kernel(tc, x, grid, w1_base, w1_spline, out):
                     w = a * BLOCKS + j
                     nc.tensor.transpose(bank[:, j, :], spline_words[:, w * P : (w + 1) * P], ident_f32[:])
                 spline_bank.append(bank)
+            idle_passes(ROUND_IDLE[r])
             base_words = base_rows[r][:].bitcast(F32)
             base_bank = banks.tile([P, rows, HALVES, P], F32, tag="bank")
             for a in range(rows):

from contextlib import ExitStack

import concourse.mybir as mybir
from concourse.masks import make_identity

BF16 = mybir.dt.bfloat16
F32 = mybir.dt.float32
U32 = mybir.dt.uint32
U8 = mybir.dt.uint8
FP8X4 = mybir.dt.float8_e4m3fn_x4
ACT = mybir.ActivationFunctionType
ALU = mybir.AluOpType

P = 128
PACK = 4
HALVES = 2
D = 512
BASES = 2
SPLINE_PASSES = D * BASES // (P * PACK)
BLOCKS = D // P
F = 1024
ROUND_ROWS = (2, 2, 2, 1, 1)
ROUNDS = len(ROUND_ROWS)
LAG = 3
BANK = 512
IDLE_COLUMNS = 256
HEAD_IDLE = 4
ROUND_IDLE = (4, 4, 4, 0, 0)

FLOPS = 2 * P * F * (D + D * BASES)


def tile_kanblock_pa_s_kernel(tc, x, grid, w1_base, w1_spline, out):
    nc = tc.nc
    x_rows = x.flatten_outer_dims()
    assert sum(ROUND_ROWS) * P == F
    first_row = [P * sum(ROUND_ROWS[:r]) for r in range(ROUNDS)]

    with ExitStack() as stack:
        stack.enter_context(tc.manual_schedule())
        const = stack.enter_context(tc.tile_pool(name="const", bufs=1))
        resident = stack.enter_context(tc.tile_pool(name="resident", bufs=ROUNDS))
        banks = stack.enter_context(tc.psum_pool(name="banks", bufs=7))
        idle = stack.enter_context(tc.psum_pool(name="idle", bufs=1))

        knots_row = const.tile([P, 4], BF16)
        nc.vector.memset(knots_row[:], 0.0)
        nc.scalar.dma_start(out=knots_row[0:1, :], in_=grid.rearrange("(o k) -> o k", o=1))
        x_sb = const.tile([P, D], BF16)
        nc.sync.dma_start(out=x_sb[:], in_=x_rows)
        base_rows = []
        spline_rows = []
        for r in range(ROUNDS):
            rows = ROUND_ROWS[r]
            these = slice(first_row[r], first_row[r] + rows * P)
            spline_sb = resident.tile([P, rows * D * BASES], BF16)
            nc.sync.dma_start(out=spline_sb[:], in_=w1_spline[these].rearrange("(p a) i g -> p (a i g)", a=rows))
            spline_rows.append(spline_sb)
            base_sb = resident.tile([P, rows * D], BF16)
            nc.sync.dma_start(out=base_sb[:], in_=w1_base[these].rearrange("(p a) k -> p (a k)", a=rows))
            base_rows.append(base_sb)

        warm = const.tile([P, 1], F32)
        nc.vector.memset(warm[:], 0.0)
        nc.scalar.activation(out=warm[:], in_=warm[:], func=ACT.Silu)
        ident_bf16 = const.tile([P, P], BF16)
        make_identity(nc, ident_bf16[:])
        ident_f32 = const.tile([P, P], F32)
        make_identity(nc, ident_f32[:])

        zero_values = const.tile([P, IDLE_COLUMNS * PACK], BF16, align_bytes=64)
        nc.vector.memset(zero_values[:], 0.0)
        zero_codes = const.tile([P, IDLE_COLUMNS], U32, align_bytes=64)
        zero_scales = const.tile([P, IDLE_COLUMNS], U8, align_bytes=64)
        nc.vector.quantize_mx(out=zero_codes[:].bitcast(FP8X4), scales=zero_scales[:], in_=zero_values[:])
        idle_bank = idle.tile([P, IDLE_COLUMNS], F32)

        def idle_passes(count):
            for i in range(count):
                nc.tensor.matmul_mx(
                    out=idle_bank[:],
                    lhsT=zero_codes[:, :P].bitcast(FP8X4),
                    lhsT_scale=zero_scales[:, :P],
                    rhs=zero_codes[:].bitcast(FP8X4),
                    rhs_scale=zero_scales[:],
                    start=True,
                    stop=True,
                )

        idle_passes(HEAD_IDLE)

        ones = const.tile([P, P], BF16)
        nc.vector.memset(ones[:], 1.0)
        knots_bank = banks.tile([P, 4], F32, tag="bank")
        nc.tensor.matmul(knots_bank[:], lhsT=ones[:], rhs=knots_row[:], start=True, stop=True)
        knots = const.tile([P, 4], F32)
        nc.vector.tensor_copy(out=knots[:], in_=knots_bank[:])
        width = const.tile([P, 2, 3], F32)
        nc.vector.tensor_sub(out=width[:, 0, :], in0=knots[:, 1:4], in1=knots[:, 0:3])
        nc.vector.tensor_sub(out=width[:, 1, :], in0=knots[:, 0:3], in1=knots[:, 1:4])
        slope = const.tile([P, 2, 3], F32)
        nc.vector.reciprocal(out=slope[:], in_=width[:])

        x_feat = banks.tile([P, BLOCKS, P], BF16, tag="bank")
        for j in range(BLOCKS):
            nc.tensor.transpose(x_feat[:, j, :], x_sb[:, j * P : (j + 1) * P], ident_bf16[:])
        x_words = banks.tile([P, HALVES, P], F32, tag="bank")
        for u in range(HALVES):
            nc.tensor.transpose(x_words[:, u, :], x_sb[:].bitcast(F32)[:, u * P : (u + 1) * P], ident_f32[:])

        silu_grouped = const.tile([P, P, PACK], BF16, align_bytes=64)
        nc.scalar.activation(
            out=silu_grouped[:].rearrange("p n (u e) -> p n u e", e=2),
            in_=x_words[:].bitcast(BF16).rearrange("p u (n e) -> p n u e", e=2),
            func=ACT.Silu,
        )

        x_clamped = const.tile([P, SPLINE_PASSES, P, HALVES], BF16)
        nc.vector.tensor_scalar(
            out=x_clamped[:],
            in0=x_feat[:].rearrange("p (g u) n -> p g n u", u=HALVES),
            scalar1=knots[:, 0:1],
            scalar2=knots[:, 3:4],
            op0=ALU.max,
            op1=ALU.min,
        )
        outer = const.tile([P, BASES, D], F32)
        inner = const.tile([P, BASES, D], F32)
        for line, e, knot, sign, m in ((inner, 0, 2, 1, 1), (inner, 1, 1, 0, 1), (outer, 0, 0, 0, 0), (outer, 1, 3, 1, 2)):
            nc.vector.tensor_scalar(
                out=line[:, e, :],
                in0=x_clamped[:].rearrange("p g n u -> p (g n u)"),
                scalar1=knots[:, knot : knot + 1],
                scalar2=slope[:, sign, m : m + 1],
                op0=ALU.subtract,
                op1=ALU.mult,
            )
        bases_grouped = const.tile([P, SPLINE_PASSES, P, PACK], BF16, align_bytes=64)
        nc.vector.scalar_tensor_tensor(
            out=bases_grouped[:].rearrange("p g n (u e) -> p (g n u) e", e=BASES),
            in0=inner[:].rearrange("p e c -> p c e"),
            scalar=0.0,
            in1=outer[:].rearrange("p e c -> p c e"),
            op0=ALU.max,
            op1=ALU.min,
        )

        silu_codes = const.tile([P, P], U32, align_bytes=64)
        silu_scales = const.tile([P, P], U8, align_bytes=64)
        bases_codes = const.tile([P, SPLINE_PASSES, P], U32, align_bytes=64)
        bases_scales = const.tile([P, SPLINE_PASSES, P], U8, align_bytes=64)

        def quantise_tokens():
            nc.vector.quantize_mx(
                out=silu_codes[:].bitcast(FP8X4),
                scales=silu_scales[:],
                in_=silu_grouped[:].rearrange("p n t -> p (n t)"),
            )
            nc.vector.quantize_mx(
                out=bases_codes[:].rearrange("p g n -> p (g n)").bitcast(FP8X4),
                scales=bases_scales[:].rearrange("p g n -> p (g n)"),
                in_=bases_grouped[:].rearrange("p g n t -> p (g n t)"),
            )

        quantised = []

        def prepare(r):
            rows = ROUND_ROWS[r]
            columns = rows * P
            spline_words = spline_rows[r][:].bitcast(F32)
            spline_bank = []
            for a in range(rows):
                bank = banks.tile([P, BLOCKS, P], F32, tag="bank")
                for j in range(BLOCKS):
                    w = a * BLOCKS + j
                    nc.tensor.transpose(bank[:, j, :], spline_words[:, w * P : (w + 1) * P], ident_f32[:])
                spline_bank.append(bank)
            idle_passes(ROUND_IDLE[r])
            base_words = base_rows[r][:].bitcast(F32)
            base_bank = banks.tile([P, rows, HALVES, P], F32, tag="bank")
            for a in range(rows):
                for u in range(HALVES):
                    w = a * HALVES + u
                    nc.tensor.transpose(base_bank[:, a, u, :], base_words[:, w * P : (w + 1) * P], ident_f32[:])

            spline_grouped = resident.tile([P, SPLINE_PASSES, columns, PACK], BF16, align_bytes=64)
            spline_grouped_words = spline_grouped[:].bitcast(F32)
            for a in range(rows):
                nc.scalar.copy(
                    out=spline_grouped_words[:, :, a * P : (a + 1) * P, :],
                    in_=spline_bank[a][:].rearrange("p (g u) f -> p g f u", u=HALVES),
                )
            base_grouped = resident.tile([P, columns, PACK], BF16, align_bytes=64)
            nc.scalar.copy(
                out=base_grouped[:].bitcast(F32).rearrange("p (a f) u -> p a f u", a=rows),
                in_=base_bank[:].rearrange("p a u f -> p a f u"),
            )

            spline_codes = resident.tile([P, SPLINE_PASSES, columns], U32, align_bytes=64)
            spline_scales = resident.tile([P, SPLINE_PASSES, columns], U8, align_bytes=64)
            nc.vector.quantize_mx(
                out=spline_codes[:].rearrange("p g f -> p (g f)").bitcast(FP8X4),
                scales=spline_scales[:].rearrange("p g f -> p (g f)"),
                in_=spline_grouped[:].rearrange("p g f t -> p (g f t)"),
            )
            base_codes = resident.tile([P, columns], U32, align_bytes=64)
            base_scales = resident.tile([P, columns], U8, align_bytes=64)
            nc.vector.quantize_mx(
                out=base_codes[:].bitcast(FP8X4),
                scales=base_scales[:],
                in_=base_grouped[:].rearrange("p f t -> p (f t)"),
            )
            quantised.append((spline_codes, spline_scales, base_codes, base_scales))

        def multiply(r):
            spline_codes, spline_scales, base_codes, base_scales = quantised[r]
            rows = ROUND_ROWS[r]
            columns = rows * P
            product = banks.tile([P, BANK], F32, tag="bank")
            for g in range(SPLINE_PASSES):
                nc.tensor.matmul_mx(
                    out=product[:, :columns],
                    lhsT=bases_codes[:, g, :].bitcast(FP8X4),
                    lhsT_scale=bases_scales[:, g, :],
                    rhs=spline_codes[:, g, :].bitcast(FP8X4),
                    rhs_scale=spline_scales[:, g, :],
                    start=(g == 0),
                    stop=False,
                )
            nc.tensor.matmul_mx(
                out=product[:, :columns],
                lhsT=silu_codes[:].bitcast(FP8X4),
                lhsT_scale=silu_scales[:],
                rhs=base_codes[:].bitcast(FP8X4),
                rhs_scale=base_scales[:],
                start=False,
                stop=True,
            )
            result = resident.tile([P, columns], F32)
            result_columns = result[:].rearrange("n (f a) -> n f a", a=rows)
            product_columns = product[:, :columns].rearrange("n (a f) -> n f a", a=rows)
            if r % 2 == 0:
                nc.vector.tensor_copy(out=result_columns, in_=product_columns)
            else:
                nc.scalar.copy(out=result_columns, in_=product_columns)
            nc.sync.dma_start(out=out[:, first_row[r] : first_row[r] + columns], in_=result[:])

        prepare(0)
        quantise_tokens()
        for r in range(1, LAG):
            prepare(r)
        for r in range(ROUNDS):
            if r + LAG < ROUNDS:
                prepare(r + LAG)
            multiply(r)
